import numpy as np
import ml_dtypes


def mxq(x, axis, fmt="e4m3"):
    dtype, down = {"e4m3": (ml_dtypes.float8_e4m3fn, 7), "e5m2": (ml_dtypes.float8_e5m2, 14)}[fmt]
    v = np.moveaxis(np.asarray(x, np.float32).astype(ml_dtypes.bfloat16).astype(np.float64), axis, -1)
    blocks = v.reshape(v.shape[:-1] + (-1, 32))
    amax = np.abs(blocks).max(-1, keepdims=True)
    byte = np.maximum(np.where(amax > 0, np.frexp(amax)[1] - 1 + 127, 0) - down, 1)
    scale = np.exp2(byte - 127.0)
    codes = (blocks / scale).astype(np.float32).astype(dtype).astype(np.float64)
    return np.moveaxis((codes * scale).reshape(v.shape), -1, axis)


WIDE = False


def mx_kscale(k):
    if not WIDE:
        return np.ones(k)
    levels = np.array([10, -10, 5, -5, 0])
    a = np.random.permutation(np.resize(levels, k // 512 * 4)).reshape(k // 512, 4)
    idx = np.arange(k)
    return np.exp2(a[idx // 512, idx % 128 // 32])


BF16 = ml_dtypes.bfloat16


def bf(x):
    return np.asarray(x, np.float32).astype(BF16)


def f64(x):
    return np.asarray(x).astype(np.float64)


B, T, DX, DY, F = 128, 5, 8192, 512, 3
MIN_CONTEXT = 1
G = 1.5 / DY ** 0.25


def setup_inputs():
    s, t = mx_kscale(DX), mx_kscale(DY)
    return {"embeddings": bf(np.random.standard_normal((B, T, DX)) * s),
            "contexts": bf(np.random.standard_normal((B, T, DY)) * G / t),
            "W": bf(np.random.standard_normal((F, DY, DX)) * G / np.sqrt(DX) * t[:, None] / s)}


def reference(embeddings, contexts, W):
    eq = mxq(f64(embeddings)[:, MIN_CONTEXT:T], 2, "e4m3")
    cq = mxq(f64(contexts)[:, MIN_CONTEXT - 1:T - 1], 2, "e4m3")
    wq = mxq(f64(W), 2, "e4m3")
    losses = []
    for step in range(F):
        S = T - step - MIN_CONTEXT
        xw = eq[:, step:] @ wq[step].T
        scores = mxq(xw, 2, "e4m3").transpose(1, 0, 2) @ cq[:, :S].transpose(1, 2, 0)
        pos = np.diagonal(scores, axis1=1, axis2=2)
        m = scores.max(2, keepdims=True)
        lse = np.log(np.exp(scores - m).sum(2)) + m[:, :, 0] - np.log(B * S)
        losses.append((lse - pos).T.reshape(-1))
    return np.concatenate(losses)

@@ -1,0 +1,251 @@
+from contextlib import ExitStack
+
+import concourse.mybir as mybir
+from concourse.masks import make_identity
+
+F32 = mybir.dt.float32
+BF16 = mybir.dt.bfloat16
+U32 = mybir.dt.uint32
+U8 = mybir.dt.uint8
+FP8X4 = mybir.dt.float8_e4m3fn_x4
+ACT = mybir.ActivationFunctionType
+ALU = mybir.AluOpType
+AXIS = mybir.AxisListType
+
+P = 128
+DX = 8192
+DY = 512
+STEPS = 3
+TIMES = 4
+PACK = 4
+K_PASS = P * PACK
+PASSES = DX // K_PASS
+BLOCKS = 4
+ROWS = BLOCKS * P
+LOAD_PASSES = 2
+LOAD_D = LOAD_PASSES * K_PASS
+PASS_WORDS = K_PASS // 2
+
+FLOPS = 2 * (4 + 3 + 2) * P * DY * DX + 2 * (4 + 3 + 2) * P * P * DY
+BYTES = 2 * (P * TIMES * DX + P * TIMES * DY + STEPS * DY * DX) + 4 * (4 + 3 + 2) * P
+
+
+def tile_infonceloss_pa_k_kernel(tc, embeddings, contexts, W, out):
+    nc = tc.nc
+    with ExitStack() as ctx:
+        consts = ctx.enter_context(tc.tile_pool(name="consts", bufs=1))
+        keep = ctx.enter_context(tc.tile_pool(name="keep", bufs=1))
+        x_loads = ctx.enter_context(tc.tile_pool(name="x_loads", bufs=3))
+        w_loads = ctx.enter_context(tc.tile_pool(name="w_loads", bufs=8))
+        stage = ctx.enter_context(tc.tile_pool(name="stage", bufs=4))
+        w_mx = ctx.enter_context(tc.tile_pool(name="w_mx", bufs=6))
+        second = ctx.enter_context(tc.tile_pool(name="second", bufs=2))
+        xw_rows = ctx.enter_context(tc.tile_pool(name="xw_rows", bufs=TIMES))
+        e_stage = ctx.enter_context(tc.tile_pool(name="e_stage", bufs=TIMES))
+        sums_psum = ctx.enter_context(tc.psum_pool(name="sums_psum", bufs=4))
+        work_psum = ctx.enter_context(tc.psum_pool(name="work_psum", bufs=4))
+        ctx.enter_context(tc.manual_schedule())
+
+        ident_f32 = consts.tile([P, P], F32)
+        make_identity(nc, ident_f32[:])
+        ident_bf16 = consts.tile([P, P], BF16)
+        make_identity(nc, ident_bf16[:])
+        ones = consts.tile([P, P], F32)
+        nc.vector.memset(ones[:], 1.0)
+
+        def load_rows(pool, rows_view, load):
+            raw = pool.tile([P, BLOCKS * LOAD_D], BF16, tag="raw")
+            nc.sync.dma_start(
+                out=raw[:].rearrange("p (r d) -> p r d", r=BLOCKS),
+                in_=rows_view[:, :, load * LOAD_D : (load + 1) * LOAD_D],
+            )
+            return raw
+
+        def turn_pass(raw, g, vector_copies_last):
+            words = raw[:].bitcast(F32)
+            grouped = stage.tile([P, ROWS * PACK], BF16, tag="grouped", align_bytes=64)
+            grouped_words = grouped[:].bitcast(F32).rearrange("p (c u) -> p c u", u=2)
+            for half in range(2):
+                bank = work_psum.tile([P, 2, 2 * P], F32, tag="work")
+                for blk in range(2):
+                    for u in range(2):
+                        first = ((2 * half + blk) * LOAD_PASSES + g % LOAD_PASSES) * PASS_WORDS + u * P
+                        nc.tensor.transpose(
+                            bank[:, u, blk * P : (blk + 1) * P], words[:, first : first + P], ident_f32[:]
+                        )
+                side_by_side = grouped_words[:, half * 2 * P : (half + 1) * 2 * P, :]
+                if half == 1 and vector_copies_last:
+                    nc.vector.tensor_copy(out=side_by_side, in_=bank[:].rearrange("p u c -> p c u"))
+                else:
+                    nc.scalar.copy(out=side_by_side, in_=bank[:].rearrange("p u c -> p c u"))
+            return grouped
+
+        def quantise(grouped, codes, scales):
+            nc.vector.quantize_mx(out=codes.bitcast(FP8X4), scales=scales, in_=grouped[:])
+
+        def turn_rows(rows):
+            turned = work_psum.tile([P, PACK, P], BF16, tag="work")
+            for t in range(PACK):
+                nc.tensor.transpose(turned[:, t, :], rows[:, t * P : (t + 1) * P], ident_bf16[:])
+            grouped = e_stage.tile([P, P * PACK], BF16, tag="grouped_e", align_bytes=64)
+            nc.vector.tensor_copy(
+                out=grouped[:].rearrange("p (r t) -> p r t", t=PACK), in_=turned[:].rearrange("p t r -> p r t")
+            )
+            return grouped
+
+        xw = {}
+        xw_codes = {}
+        xw_scales = {}
+        loss = {}
+
+        def round_xw(k):
+            xw_codes[k] = second.tile([P, TIMES * P], U32, tag="xw_codes", align_bytes=64, name="xw_codes_%d" % k)
+            xw_scales[k] = second.tile([P, TIMES * P], U8, tag="xw_scales", align_bytes=64, name="xw_scales_%d" % k)
+            for s in range(TIMES - k):
+                xw[(k, s)] = xw_rows.tile([P, DY], BF16, tag="xw", name="xw_%d_%d" % (k, s))
+                if s % 2 == 0:
+                    nc.scalar.copy(out=xw[(k, s)][:], in_=sums[(k, s)][:])
+                else:
+                    nc.vector.tensor_copy(out=xw[(k, s)][:], in_=sums[(k, s)][:])
+
+        def turn_xw(k, s):
+            cols = slice(s * P, (s + 1) * P)
+            return (turn_rows(xw[(k, s)]), xw_codes[k][:, cols], xw_scales[k][:, cols])
+
+        def scores_to_loss(k):
+            n_s = TIMES - k
+            scores = work_psum.tile([P, n_s, P], F32, tag="work")
+            for s in range(n_s):
+                cols = slice(s * P, (s + 1) * P)
+                nc.tensor.matmul_mx(
+                    out=scores[:, s, :],
+                    lhsT=xw_codes[k][:, cols].bitcast(FP8X4),
+                    lhsT_scale=xw_scales[k][:, cols],
+                    rhs=c_codes[:, cols].bitcast(FP8X4),
+                    rhs_scale=c_scales[:, cols],
+                    start=True,
+                    stop=True,
+                )
+            top = second.tile([P, n_s], F32, tag="top")
+            nc.vector.tensor_reduce(out=top[:], in_=scores[:], axis=AXIS.X, op=ALU.max)
+            minus_top = second.tile([P, n_s], F32, tag="minus_top")
+            nc.vector.tensor_scalar_mul(out=minus_top[:], in0=top[:], scalar1=-1.0)
+            on_diagonal = second.tile([P, n_s, P], F32, tag="on_diagonal")
+            nc.vector.tensor_tensor(
+                out=on_diagonal[:],
+                in0=scores[:],
+                in1=ident_f32[:].unsqueeze(1).to_broadcast([P, n_s, P]),
+                op=ALU.mult,
+            )
+            exps = second.tile([P, n_s, P], F32, tag="exps")
+            exp_sums = second.tile([P, n_s], F32, tag="exp_sums")
+            for s in range(n_s):
+                nc.scalar.activation(
+                    out=exps[:, s, :],
+                    in_=scores[:, s, :],
+                    func=ACT.Exp,
+                    bias=minus_top[:, s : s + 1],
+                    scale=1.0,
+                    accum_out=exp_sums[:, s : s + 1],
+                )
+            positive = second.tile([P, n_s], F32, tag="positive")
+            nc.vector.tensor_reduce(out=positive[:], in_=on_diagonal[:], axis=AXIS.X, op=ALU.add)
+            top_less_positive = second.tile([P, n_s], F32, tag="top_less_positive")
+            nc.vector.tensor_sub(out=top_less_positive[:], in0=top[:], in1=positive[:])
+            log_mean = second.tile([P, n_s], F32, tag="log_mean")
+            nc.scalar.activation(out=log_mean[:], in_=exp_sums[:], func=ACT.Ln, scale=1.0 / (P * n_s))
+            loss[k] = second.tile([P, n_s], F32, tag="loss", name="loss_%d" % k)
+            nc.vector.tensor_add(out=loss[k][:], in0=log_mean[:], in1=top_less_positive[:])
+
+        def store_loss(k):
+            n_s = TIMES - k
+            spread = second.tile([P, P, n_s], F32, tag="spread")
+            nc.vector.tensor_tensor(
+                out=spread[:],
+                in0=ident_f32[:].unsqueeze(2).to_broadcast([P, P, n_s]),
+                in1=loss[k][:].unsqueeze(1).to_broadcast([P, P, n_s]),
+                op=ALU.mult,
+            )
+            run_psum = work_psum.tile([P, P * n_s], F32, tag="work")
+            nc.tensor.matmul(
+                out=run_psum[:], lhsT=ones[:], rhs=spread[:].rearrange("p b s -> p (b s)"), start=True, stop=True
+            )
+            run = second.tile([P, P * n_s], F32, tag="run")
+            nc.scalar.copy(out=run[:], in_=run_psum[:])
+            first = sum(P * (TIMES - j) for j in range(k))
+            nc.scalar.dma_start(
+                out=out[first : first + P * n_s].rearrange("(o n) -> o n", o=1), in_=run[0:1, :]
+            )
+
+        c_raw = keep.tile([P, TIMES * DY], BF16)
+        nc.sync.dma_start(out=c_raw[:].rearrange("p (t e) -> p t e", t=TIMES), in_=contexts[:, 0:TIMES, :])
+        c_codes = keep.tile([P, TIMES * P], U32, align_bytes=64)
+        c_scales = keep.tile([P, TIMES * P], U8, align_bytes=64)
+        c_turned = [turn_rows(c_raw[:, s * DY : (s + 1) * DY]) for s in range(TIMES)]
+        for s in range(TIMES):
+            cols = slice(s * P, (s + 1) * P)
+            quantise(c_turned[s], c_codes[:, cols], c_scales[:, cols])
+
+        x_view = embeddings[:, 1 : 1 + TIMES, :]
+        x_codes = keep.tile([P, PASSES * ROWS], U32, align_bytes=64)
+        x_scales = keep.tile([P, PASSES * ROWS], U8, align_bytes=64)
+        sums = {}
+
+        def multiply(k, g, w_codes, w_scales):
+            for s in range(TIMES - k):
+                if g == 0:
+                    sums[(k, s)] = sums_psum.tile([P, DY], F32, tag="sums", name="sums_%d_%d" % (k, s))
+                cols = slice(g * ROWS + (k + s) * P, g * ROWS + (k + s + 1) * P)
+                nc.tensor.matmul_mx(
+                    out=sums[(k, s)][:],
+                    lhsT=x_codes[:, cols].bitcast(FP8X4),
+                    lhsT_scale=x_scales[:, cols],
+                    rhs=w_codes[:].bitcast(FP8X4),
+                    rhs_scale=w_scales[:],
+                    start=(g == 0),
+                    stop=(g == PASSES - 1),
+                )
+
+        waiting = []
+        for k in range(STEPS):
+            w_view = W[k].rearrange("(r p) d -> p r d", p=P)
+            w_passes = 1 if k == 0 else 2
+            n_before = TIMES - (k - 1)
+            for rnd in range(PASSES // w_passes):
+                turned = []
+                if k == 0:
+                    g = rnd
+                    if g % LOAD_PASSES == 0:
+                        x_raw = load_rows(x_loads, x_view, g // LOAD_PASSES)
+                    cols = slice(g * ROWS, (g + 1) * ROWS)
+                    turned.append((turn_pass(x_raw, g, False), x_codes[:, cols], x_scales[:, cols]))
+                ready = []
+                for g in range(rnd * w_passes, (rnd + 1) * w_passes):
+                    if g % LOAD_PASSES == 0:
+                        w_raw = load_rows(w_loads, w_view, g // LOAD_PASSES)
+                    w_codes = w_mx.tile([P, ROWS], U32, tag="w_codes", align_bytes=64)
+                    w_scales = w_mx.tile([P, ROWS], U8, tag="w_scales", align_bytes=64)
+                    turned.append((turn_pass(w_raw, g, len(turned) == 1), w_codes[:], w_scales[:]))
+                    ready.append((k, g, w_codes, w_scales))
+                if k > 0 and 1 <= rnd <= n_before:
+                    turned.append(turn_xw(k - 1, rnd - 1))
+                for grouped, codes, scales in turned:
+                    quantise(grouped, codes, scales)
+                for item in waiting:
+                    multiply(*item)
+                waiting = ready
+                if k > 0 and rnd == 0:
+                    round_xw(k - 1)
+                if k > 0 and rnd == n_before + 1:
+                    scores_to_loss(k - 1)
+                if k > 0 and rnd == n_before + 3:
+                    store_loss(k - 1)
+
+        for item in waiting:
+            multiply(*item)
+        last = STEPS - 1
+        round_xw(last)
+        for grouped, codes, scales in [turn_xw(last, s) for s in range(TIMES - last)]:
+            quantise(grouped, codes, scales)
+        scores_to_loss(last)
+        store_loss(last)

@@ -25,6 +25,8 @@ ROWS = BLOCKS * P
 LOAD_PASSES = 2
 LOAD_D = LOAD_PASSES * K_PASS
 PASS_WORDS = K_PASS // 2
+LAG = 2
+SPARE = "sums3"
 
 FLOPS = 2 * (4 + 3 + 2) * P * DY * DX + 2 * (4 + 3 + 2) * P * P * DY
 BYTES = 2 * (P * TIMES * DX + P * TIMES * DY + STEPS * DY * DX) + 4 * (4 + 3 + 2) * P
@@ -38,11 +40,11 @@ def tile_infonceloss_pa_k_kernel(tc, embeddings, contexts, W, out):
         x_loads = ctx.enter_context(tc.tile_pool(name="x_loads", bufs=3))
         w_loads = ctx.enter_context(tc.tile_pool(name="w_loads", bufs=8))
         stage = ctx.enter_context(tc.tile_pool(name="stage", bufs=4))
-        w_mx = ctx.enter_context(tc.tile_pool(name="w_mx", bufs=6))
+        w_mx = ctx.enter_context(tc.tile_pool(name="w_mx", bufs=2 * (LAG + 2)))
         second = ctx.enter_context(tc.tile_pool(name="second", bufs=2))
         xw_rows = ctx.enter_context(tc.tile_pool(name="xw_rows", bufs=TIMES))
         e_stage = ctx.enter_context(tc.tile_pool(name="e_stage", bufs=TIMES))
-        sums_psum = ctx.enter_context(tc.psum_pool(name="sums_psum", bufs=4))
+        sums_psum = ctx.enter_context(tc.psum_pool(name="sums_psum", bufs=1))
         work_psum = ctx.enter_context(tc.psum_pool(name="work_psum", bufs=4))
         ctx.enter_context(tc.manual_schedule())
 
@@ -52,6 +54,8 @@ def tile_infonceloss_pa_k_kernel(tc, embeddings, contexts, W, out):
         make_identity(nc, ident_bf16[:])
         ones = consts.tile([P, P], F32)
         nc.vector.memset(ones[:], 1.0)
+        warm = consts.tile([P, 1], F32)
+        nc.scalar.activation(out=warm[:], in_=ones[:, 0:1], func=ACT.Exp)
 
         def load_rows(pool, rows_view, load):
             raw = pool.tile([P, BLOCKS * LOAD_D], BF16, tag="raw")
@@ -83,20 +87,28 @@ def tile_infonceloss_pa_k_kernel(tc, embeddings, contexts, W, out):
         def quantise(grouped, codes, scales):
             nc.vector.quantize_mx(out=codes.bitcast(FP8X4), scales=scales, in_=grouped[:])
 
-        def turn_rows(rows):
+        def turn_rows(rows, on_scalar):
             turned = work_psum.tile([P, PACK, P], BF16, tag="work")
             for t in range(PACK):
                 nc.tensor.transpose(turned[:, t, :], rows[:, t * P : (t + 1) * P], ident_bf16[:])
             grouped = e_stage.tile([P, P * PACK], BF16, tag="grouped_e", align_bytes=64)
-            nc.vector.tensor_copy(
-                out=grouped[:].rearrange("p (r t) -> p r t", t=PACK), in_=turned[:].rearrange("p t r -> p r t")
-            )
+            side_by_side = grouped[:].rearrange("p (r t) -> p r t", t=PACK)
+            if on_scalar:
+                nc.scalar.copy(out=side_by_side, in_=turned[:].rearrange("p t r -> p r t"))
+            else:
+                nc.vector.tensor_copy(out=side_by_side, in_=turned[:].rearrange("p t r -> p r t"))
             return grouped
 
         xw = {}
         xw_codes = {}
         xw_scales = {}
-        loss = {}
+        scores = {}
+        minus_top = {}
+        top_less_positive = {}
+        exp_sums = {}
+        log_mean = {}
+        spread = {}
+        run_psum = {}
 
         def round_xw(k):
             xw_codes[k] = second.tile([P, TIMES * P], U32, tag="xw_codes", align_bytes=64, name="xw_codes_%d" % k)
@@ -110,15 +122,15 @@ def tile_infonceloss_pa_k_kernel(tc, embeddings, contexts, W, out):
 
         def turn_xw(k, s):
             cols = slice(s * P, (s + 1) * P)
-            return (turn_rows(xw[(k, s)]), xw_codes[k][:, cols], xw_scales[k][:, cols])
+            return (turn_rows(xw[(k, s)], s % 2 == 0), xw_codes[k][:, cols], xw_scales[k][:, cols])
 
-        def scores_to_loss(k):
+        def score(k):
             n_s = TIMES - k
-            scores = work_psum.tile([P, n_s, P], F32, tag="work")
+            scores[k] = sums_psum.tile([P, n_s, P], F32, tag=SPARE, name="scores_%d" % k)
             for s in range(n_s):
                 cols = slice(s * P, (s + 1) * P)
                 nc.tensor.matmul_mx(
-                    out=scores[:, s, :],
+                    out=scores[k][:, s, :],
                     lhsT=xw_codes[k][:, cols].bitcast(FP8X4),
                     lhsT_scale=xw_scales[k][:, cols],
                     rhs=c_codes[:, cols].bitcast(FP8X4),
@@ -127,61 +139,70 @@ def tile_infonceloss_pa_k_kernel(tc, embeddings, contexts, W, out):
                     stop=True,
                 )
             top = second.tile([P, n_s], F32, tag="top")
-            nc.vector.tensor_reduce(out=top[:], in_=scores[:], axis=AXIS.X, op=ALU.max)
-            minus_top = second.tile([P, n_s], F32, tag="minus_top")
-            nc.vector.tensor_scalar_mul(out=minus_top[:], in0=top[:], scalar1=-1.0)
+            nc.vector.tensor_reduce(out=top[:], in_=scores[k][:], axis=AXIS.X, op=ALU.max)
+            minus_top[k] = second.tile([P, n_s], F32, tag="minus_top", name="minus_top_%d" % k)
+            nc.vector.tensor_scalar_mul(out=minus_top[k][:], in0=top[:], scalar1=-1.0)
             on_diagonal = second.tile([P, n_s, P], F32, tag="on_diagonal")
             nc.vector.tensor_tensor(
                 out=on_diagonal[:],
-                in0=scores[:],
+                in0=scores[k][:],
                 in1=ident_f32[:].unsqueeze(1).to_broadcast([P, n_s, P]),
                 op=ALU.mult,
             )
+            positive = second.tile([P, n_s], F32, tag="positive")
+            nc.vector.tensor_reduce(out=positive[:], in_=on_diagonal[:], axis=AXIS.X, op=ALU.add)
+            top_less_positive[k] = second.tile([P, n_s], F32, tag="top_less_positive", name="tlp_%d" % k)
+            nc.vector.tensor_sub(out=top_less_positive[k][:], in0=top[:], in1=positive[:])
+
+        def exponentials(k):
+            n_s = TIMES - k
             exps = second.tile([P, n_s, P], F32, tag="exps")
-            exp_sums = second.tile([P, n_s], F32, tag="exp_sums")
+            exp_sums[k] = second.tile([P, n_s], F32, tag="exp_sums", name="exp_sums_%d" % k)
             for s in range(n_s):
                 nc.scalar.activation(
                     out=exps[:, s, :],
-                    in_=scores[:, s, :],
+                    in_=scores[k][:, s, :],
                     func=ACT.Exp,
-                    bias=minus_top[:, s : s + 1],
+                    bias=minus_top[k][:, s : s + 1],
                     scale=1.0,
-                    accum_out=exp_sums[:, s : s + 1],
+                    accum_out=exp_sums[k][:, s : s + 1],
                 )
-            positive = second.tile([P, n_s], F32, tag="positive")
-            nc.vector.tensor_reduce(out=positive[:], in_=on_diagonal[:], axis=AXIS.X, op=ALU.add)
-            top_less_positive = second.tile([P, n_s], F32, tag="top_less_positive")
-            nc.vector.tensor_sub(out=top_less_positive[:], in0=top[:], in1=positive[:])
-            log_mean = second.tile([P, n_s], F32, tag="log_mean")
-            nc.scalar.activation(out=log_mean[:], in_=exp_sums[:], func=ACT.Ln, scale=1.0 / (P * n_s))
-            loss[k] = second.tile([P, n_s], F32, tag="loss", name="loss_%d" % k)
-            nc.vector.tensor_add(out=loss[k][:], in0=log_mean[:], in1=top_less_positive[:])
 
-        def store_loss(k):
+        def logarithm(k):
             n_s = TIMES - k
-            spread = second.tile([P, P, n_s], F32, tag="spread")
+            log_mean[k] = second.tile([P, n_s], F32, tag="log_mean", name="log_mean_%d" % k)
+            nc.scalar.activation(out=log_mean[k][:], in_=exp_sums[k][:], func=ACT.Ln, scale=1.0 / (P * n_s))
+
+        def spread_loss(k):
+            n_s = TIMES - k
+            loss = second.tile([P, n_s], F32, tag="loss")
+            nc.vector.tensor_add(out=loss[:], in0=log_mean[k][:], in1=top_less_positive[k][:])
+            spread[k] = second.tile([P, P, n_s], F32, tag="spread", name="spread_%d" % k)
             nc.vector.tensor_tensor(
-                out=spread[:],
+                out=spread[k][:],
                 in0=ident_f32[:].unsqueeze(2).to_broadcast([P, P, n_s]),
-                in1=loss[k][:].unsqueeze(1).to_broadcast([P, P, n_s]),
+                in1=loss[:].unsqueeze(1).to_broadcast([P, P, n_s]),
                 op=ALU.mult,
             )
-            run_psum = work_psum.tile([P, P * n_s], F32, tag="work")
+
+        def flatten(k):
+            run_psum[k] = sums_psum.tile([P, P * (TIMES - k)], F32, tag=SPARE, name="run_psum_%d" % k)
             nc.tensor.matmul(
-                out=run_psum[:], lhsT=ones[:], rhs=spread[:].rearrange("p b s -> p (b s)"), start=True, stop=True
+                out=run_psum[k][:], lhsT=ones[:], rhs=spread[k][:].rearrange("p b s -> p (b s)"), start=True, stop=True
             )
-            run = second.tile([P, P * n_s], F32, tag="run")
-            nc.scalar.copy(out=run[:], in_=run_psum[:])
+
+        def store(k):
+            n = P * (TIMES - k)
+            run = second.tile([P, n], F32, tag="run")
+            nc.scalar.copy(out=run[:], in_=run_psum[k][:])
             first = sum(P * (TIMES - j) for j in range(k))
-            nc.scalar.dma_start(
-                out=out[first : first + P * n_s].rearrange("(o n) -> o n", o=1), in_=run[0:1, :]
-            )
+            nc.scalar.dma_start(out=out[first : first + n].rearrange("(o n) -> o n", o=1), in_=run[0:1, :])
 
         c_raw = keep.tile([P, TIMES * DY], BF16)
         nc.sync.dma_start(out=c_raw[:].rearrange("p (t e) -> p t e", t=TIMES), in_=contexts[:, 0:TIMES, :])
         c_codes = keep.tile([P, TIMES * P], U32, align_bytes=64)
         c_scales = keep.tile([P, TIMES * P], U8, align_bytes=64)
-        c_turned = [turn_rows(c_raw[:, s * DY : (s + 1) * DY]) for s in range(TIMES)]
+        c_turned = [turn_rows(c_raw[:, s * DY : (s + 1) * DY], s % 2 == 0) for s in range(TIMES)]
         for s in range(TIMES):
             cols = slice(s * P, (s + 1) * P)
             quantise(c_turned[s], c_codes[:, cols], c_scales[:, cols])
@@ -194,7 +215,7 @@ def tile_infonceloss_pa_k_kernel(tc, embeddings, contexts, W, out):
         def multiply(k, g, w_codes, w_scales):
             for s in range(TIMES - k):
                 if g == 0:
-                    sums[(k, s)] = sums_psum.tile([P, DY], F32, tag="sums", name="sums_%d_%d" % (k, s))
+                    sums[(k, s)] = sums_psum.tile([P, DY], F32, tag="sums%d" % s, name="sums_%d_%d" % (k, s))
                 cols = slice(g * ROWS + (k + s) * P, g * ROWS + (k + s + 1) * P)
                 nc.tensor.matmul_mx(
                     out=sums[(k, s)][:],
@@ -206,46 +227,56 @@ def tile_infonceloss_pa_k_kernel(tc, embeddings, contexts, W, out):
                     stop=(g == PASSES - 1),
                 )
 
-        waiting = []
+        plan = []
         for k in range(STEPS):
-            w_view = W[k].rearrange("(r p) d -> p r d", p=P)
             w_passes = 1 if k == 0 else 2
-            n_before = TIMES - (k - 1)
-            for rnd in range(PASSES // w_passes):
-                turned = []
+            for first in range(0, PASSES, w_passes):
+                plan.append((k, range(first, first + w_passes)))
+
+        quantised = {}
+        closed_in = {}
+        for rnd in range(len(plan) + LAG + TIMES + 7):
+            turned = []
+            quantised[rnd] = []
+            if rnd < len(plan):
+                k, w_passes = plan[rnd]
                 if k == 0:
                     g = rnd
                     if g % LOAD_PASSES == 0:
                         x_raw = load_rows(x_loads, x_view, g // LOAD_PASSES)
                     cols = slice(g * ROWS, (g + 1) * ROWS)
                     turned.append((turn_pass(x_raw, g, False), x_codes[:, cols], x_scales[:, cols]))
-                ready = []
-                for g in range(rnd * w_passes, (rnd + 1) * w_passes):
+                for g in w_passes:
                     if g % LOAD_PASSES == 0:
+                        w_view = W[k].rearrange("(r p) d -> p r d", p=P)
                         w_raw = load_rows(w_loads, w_view, g // LOAD_PASSES)
                     w_codes = w_mx.tile([P, ROWS], U32, tag="w_codes", align_bytes=64)
                     w_scales = w_mx.tile([P, ROWS], U8, tag="w_scales", align_bytes=64)
                     turned.append((turn_pass(w_raw, g, len(turned) == 1), w_codes[:], w_scales[:]))
-                    ready.append((k, g, w_codes, w_scales))
-                if k > 0 and 1 <= rnd <= n_before:
-                    turned.append(turn_xw(k - 1, rnd - 1))
-                for grouped, codes, scales in turned:
-                    quantise(grouped, codes, scales)
-                for item in waiting:
-                    multiply(*item)
-                waiting = ready
-                if k > 0 and rnd == 0:
-                    round_xw(k - 1)
-                if k > 0 and rnd == n_before + 1:
-                    scores_to_loss(k - 1)
-                if k > 0 and rnd == n_before + 3:
-                    store_loss(k - 1)
-
-        for item in waiting:
-            multiply(*item)
-        last = STEPS - 1
-        round_xw(last)
-        for grouped, codes, scales in [turn_xw(last, s) for s in range(TIMES - last)]:
-            quantise(grouped, codes, scales)
-        scores_to_loss(last)
-        store_loss(last)
+                    quantised[rnd].append((k, g, w_codes, w_scales))
+            for done in sorted(closed_in):
+                s = rnd - closed_in[done] - 1
+                if 0 <= s < TIMES - done:
+                    turned.append(turn_xw(done, s))
+            for grouped, codes, scales in turned:
+                quantise(grouped, codes, scales)
+            for k, g, w_codes, w_scales in quantised.get(rnd - LAG, []):
+                multiply(k, g, w_codes, w_scales)
+                if g == PASSES - 1:
+                    closed_in[k] = rnd
+            for done in sorted(closed_in):
+                if rnd == closed_in[done]:
+                    round_xw(done)
+                since_turned = rnd - closed_in[done] - (TIMES - done)
+                if since_turned == 1:
+                    score(done)
+                if since_turned == 2:
+                    exponentials(done)
+                if since_turned == 3:
+                    logarithm(done)
+                if since_turned == 4:
+                    spread_loss(done)
+                if since_turned == 5:
+                    flatten(done)
+                if since_turned == 6:
+                    store(done)

@@ -26,7 +26,7 @@ LOAD_PASSES = 2
 LOAD_D = LOAD_PASSES * K_PASS
 PASS_WORDS = K_PASS // 2
 LAG = 2
-SPARE = "sums3"
+GATHER = 8
 
 FLOPS = 2 * (4 + 3 + 2) * P * DY * DX + 2 * (4 + 3 + 2) * P * P * DY
 BYTES = 2 * (P * TIMES * DX + P * TIMES * DY + STEPS * DY * DX) + 4 * (4 + 3 + 2) * P
@@ -43,7 +43,7 @@ def tile_infonceloss_pa_k_kernel(tc, embeddings, contexts, W, out):
         w_mx = ctx.enter_context(tc.tile_pool(name="w_mx", bufs=2 * (LAG + 2)))
         second = ctx.enter_context(tc.tile_pool(name="second", bufs=2))
         xw_rows = ctx.enter_context(tc.tile_pool(name="xw_rows", bufs=TIMES))
-        e_stage = ctx.enter_context(tc.tile_pool(name="e_stage", bufs=TIMES))
+        e_stage = ctx.enter_context(tc.tile_pool(name="e_stage", bufs=2))
         sums_psum = ctx.enter_context(tc.psum_pool(name="sums_psum", bufs=1))
         work_psum = ctx.enter_context(tc.psum_pool(name="work_psum", bufs=4))
         ctx.enter_context(tc.manual_schedule())
@@ -52,10 +52,20 @@ def tile_infonceloss_pa_k_kernel(tc, embeddings, contexts, W, out):
         make_identity(nc, ident_f32[:])
         ident_bf16 = consts.tile([P, P], BF16)
         make_identity(nc, ident_bf16[:])
-        ones = consts.tile([P, P], F32)
-        nc.vector.memset(ones[:], 1.0)
+        group = consts.tile([P, P], F32)
+        nc.vector.memset(group[:], 0.0)
+        nc.vector.tensor_reduce(
+            out=group[:, 0 : P // GATHER],
+            in_=ident_f32[:].rearrange("p (h l) -> p h l", l=GATHER),
+            axis=AXIS.X,
+            op=ALU.add,
+        )
+        place = consts.tile([P, GATHER], F32)
+        nc.vector.tensor_reduce(
+            out=place[:], in_=ident_f32[:].rearrange("p (h l) -> p l h", l=GATHER), axis=AXIS.X, op=ALU.add
+        )
         warm = consts.tile([P, 1], F32)
-        nc.scalar.activation(out=warm[:], in_=ones[:, 0:1], func=ACT.Exp)
+        nc.scalar.activation(out=warm[:], in_=place[:, 0:1], func=ACT.Exp)
 
         def load_rows(pool, rows_view, load):
             raw = pool.tile([P, BLOCKS * LOAD_D], BF16, tag="raw")
@@ -87,28 +97,37 @@ def tile_infonceloss_pa_k_kernel(tc, embeddings, contexts, W, out):
         def quantise(grouped, codes, scales):
             nc.vector.quantize_mx(out=codes.bitcast(FP8X4), scales=scales, in_=grouped[:])
 
-        def turn_rows(rows, on_scalar):
-            turned = work_psum.tile([P, PACK, P], BF16, tag="work")
-            for t in range(PACK):
-                nc.tensor.transpose(turned[:, t, :], rows[:, t * P : (t + 1) * P], ident_bf16[:])
-            grouped = e_stage.tile([P, P * PACK], BF16, tag="grouped_e", align_bytes=64)
-            side_by_side = grouped[:].rearrange("p (r t) -> p r t", t=PACK)
+        def turn_rows(rows_list, bank, on_scalar):
+            n = len(rows_list)
+            turned = sums_psum.tile([P, n, PACK, P], BF16, tag=bank)
+            for i in range(n):
+                for t in range(PACK):
+                    nc.tensor.transpose(turned[:, i, t, :], rows_list[i][:, t * P : (t + 1) * P], ident_bf16[:])
+            grouped = e_stage.tile([P, n * P * PACK], BF16, tag="grouped_e", align_bytes=64)
+            side_by_side = grouped[:].rearrange("p (i r t) -> p i r t", i=n, t=PACK)
             if on_scalar:
-                nc.scalar.copy(out=side_by_side, in_=turned[:].rearrange("p t r -> p r t"))
+                nc.scalar.copy(out=side_by_side, in_=turned[:].rearrange("p i t r -> p i r t"))
             else:
-                nc.vector.tensor_copy(out=side_by_side, in_=turned[:].rearrange("p t r -> p r t"))
+                nc.vector.tensor_copy(out=side_by_side, in_=turned[:].rearrange("p i t r -> p i r t"))
             return grouped
+
+        def own_bank(k):
+            return "sums%d" % (TIMES - 1 - k)
+
+        def pairs(k):
+            return (TIMES - k + 1) // 2
 
         xw = {}
         xw_codes = {}
         xw_scales = {}
         scores = {}
+        top = {}
         minus_top = {}
         top_less_positive = {}
         exp_sums = {}
         log_mean = {}
-        spread = {}
-        run_psum = {}
+        placed = {}
+        gathered = {}
 
         def round_xw(k):
             xw_codes[k] = second.tile([P, TIMES * P], U32, tag="xw_codes", align_bytes=64, name="xw_codes_%d" % k)
@@ -120,13 +139,15 @@ def tile_infonceloss_pa_k_kernel(tc, embeddings, contexts, W, out):
                 else:
                     nc.vector.tensor_copy(out=xw[(k, s)][:], in_=sums[(k, s)][:])
 
-        def turn_xw(k, s):
-            cols = slice(s * P, (s + 1) * P)
-            return (turn_rows(xw[(k, s)], s % 2 == 0), xw_codes[k][:, cols], xw_scales[k][:, cols])
+        def turn_xw(k, pair):
+            times = range(2 * pair, min(2 * pair + 2, TIMES - k))
+            cols = slice(times[0] * P, (times[-1] + 1) * P)
+            grouped = turn_rows([xw[(k, s)] for s in times], own_bank(k), pair % 2 == 1)
+            return (grouped, xw_codes[k][:, cols], xw_scales[k][:, cols])
 
         def score(k):
             n_s = TIMES - k
-            scores[k] = sums_psum.tile([P, n_s, P], F32, tag=SPARE, name="scores_%d" % k)
+            scores[k] = sums_psum.tile([P, n_s, P], F32, tag=own_bank(k), name="scores_%d" % k)
             for s in range(n_s):
                 cols = slice(s * P, (s + 1) * P)
                 nc.tensor.matmul_mx(
@@ -138,10 +159,13 @@ def tile_infonceloss_pa_k_kernel(tc, embeddings, contexts, W, out):
                     start=True,
                     stop=True,
                 )
-            top = second.tile([P, n_s], F32, tag="top")
-            nc.vector.tensor_reduce(out=top[:], in_=scores[k][:], axis=AXIS.X, op=ALU.max)
+            top[k] = second.tile([P, n_s], F32, tag="top", name="top_%d" % k)
+            nc.vector.tensor_reduce(out=top[k][:], in_=scores[k][:], axis=AXIS.X, op=ALU.max)
             minus_top[k] = second.tile([P, n_s], F32, tag="minus_top", name="minus_top_%d" % k)
-            nc.vector.tensor_scalar_mul(out=minus_top[k][:], in0=top[:], scalar1=-1.0)
+            nc.vector.tensor_scalar_mul(out=minus_top[k][:], in0=top[k][:], scalar1=-1.0)
+
+        def diagonal(k):
+            n_s = TIMES - k
             on_diagonal = second.tile([P, n_s, P], F32, tag="on_diagonal")
             nc.vector.tensor_tensor(
                 out=on_diagonal[:],
@@ -152,7 +176,7 @@ def tile_infonceloss_pa_k_kernel(tc, embeddings, contexts, W, out):
             positive = second.tile([P, n_s], F32, tag="positive")
             nc.vector.tensor_reduce(out=positive[:], in_=on_diagonal[:], axis=AXIS.X, op=ALU.add)
             top_less_positive[k] = second.tile([P, n_s], F32, tag="top_less_positive", name="tlp_%d" % k)
-            nc.vector.tensor_sub(out=top_less_positive[k][:], in0=top[:], in1=positive[:])
+            nc.vector.tensor_sub(out=top_less_positive[k][:], in0=top[k][:], in1=positive[:])
 
         def exponentials(k):
             n_s = TIMES - k
@@ -173,39 +197,41 @@ def tile_infonceloss_pa_k_kernel(tc, embeddings, contexts, W, out):
             log_mean[k] = second.tile([P, n_s], F32, tag="log_mean", name="log_mean_%d" % k)
             nc.scalar.activation(out=log_mean[k][:], in_=exp_sums[k][:], func=ACT.Ln, scale=1.0 / (P * n_s))
 
-        def spread_loss(k):
+        def place_loss(k):
             n_s = TIMES - k
             loss = second.tile([P, n_s], F32, tag="loss")
             nc.vector.tensor_add(out=loss[:], in0=log_mean[k][:], in1=top_less_positive[k][:])
-            spread[k] = second.tile([P, P, n_s], F32, tag="spread", name="spread_%d" % k)
+            placed[k] = second.tile([P, GATHER, n_s], F32, tag="placed", name="placed_%d" % k)
             nc.vector.tensor_tensor(
-                out=spread[k][:],
-                in0=ident_f32[:].unsqueeze(2).to_broadcast([P, P, n_s]),
-                in1=loss[:].unsqueeze(1).to_broadcast([P, P, n_s]),
+                out=placed[k][:],
+                in0=place[:].unsqueeze(2).to_broadcast([P, GATHER, n_s]),
+                in1=loss[:].unsqueeze(1).to_broadcast([P, GATHER, n_s]),
                 op=ALU.mult,
             )
 
-        def flatten(k):
-            run_psum[k] = sums_psum.tile([P, P * (TIMES - k)], F32, tag=SPARE, name="run_psum_%d" % k)
+        def gather(k):
+            gathered[k] = sums_psum.tile([P, GATHER * (TIMES - k)], F32, tag=own_bank(k), name="gathered_%d" % k)
             nc.tensor.matmul(
-                out=run_psum[k][:], lhsT=ones[:], rhs=spread[k][:].rearrange("p b s -> p (b s)"), start=True, stop=True
+                out=gathered[k][:], lhsT=group[:], rhs=placed[k][:].rearrange("p l s -> p (l s)"), start=True, stop=True
             )
 
         def store(k):
-            n = P * (TIMES - k)
-            run = second.tile([P, n], F32, tag="run")
-            nc.scalar.copy(out=run[:], in_=run_psum[k][:])
+            groups = P // GATHER
+            n = GATHER * (TIMES - k)
+            runs = second.tile([groups, n], F32, tag="runs")
+            nc.scalar.copy(out=runs[:], in_=gathered[k][0:groups, :])
             first = sum(P * (TIMES - j) for j in range(k))
-            nc.scalar.dma_start(out=out[first : first + n].rearrange("(o n) -> o n", o=1), in_=run[0:1, :])
+            nc.scalar.dma_start(out=out[first : first + groups * n].rearrange("(h n) -> h n", h=groups), in_=runs[:])
 
         c_raw = keep.tile([P, TIMES * DY], BF16)
         nc.sync.dma_start(out=c_raw[:].rearrange("p (t e) -> p t e", t=TIMES), in_=contexts[:, 0:TIMES, :])
         c_codes = keep.tile([P, TIMES * P], U32, align_bytes=64)
         c_scales = keep.tile([P, TIMES * P], U8, align_bytes=64)
-        c_turned = [turn_rows(c_raw[:, s * DY : (s + 1) * DY], s % 2 == 0) for s in range(TIMES)]
-        for s in range(TIMES):
-            cols = slice(s * P, (s + 1) * P)
-            quantise(c_turned[s], c_codes[:, cols], c_scales[:, cols])
+        c_rows = [c_raw[:, s * DY : (s + 1) * DY] for s in range(TIMES)]
+        c_turned = [turn_rows(c_rows[2 * pair : 2 * pair + 2], "sums%d" % pair, pair % 2 == 1) for pair in range(2)]
+        for pair in range(2):
+            cols = slice(2 * pair * P, 2 * (pair + 1) * P)
+            quantise(c_turned[pair], c_codes[:, cols], c_scales[:, cols])
 
         x_view = embeddings[:, 1 : 1 + TIMES, :]
         x_codes = keep.tile([P, PASSES * ROWS], U32, align_bytes=64)
@@ -255,9 +281,9 @@ def tile_infonceloss_pa_k_kernel(tc, embeddings, contexts, W, out):
                     turned.append((turn_pass(w_raw, g, len(turned) == 1), w_codes[:], w_scales[:]))
                     quantised[rnd].append((k, g, w_codes, w_scales))
             for done in sorted(closed_in):
-                s = rnd - closed_in[done] - 1
-                if 0 <= s < TIMES - done:
-                    turned.append(turn_xw(done, s))
+                pair = rnd - closed_in[done] - 1
+                if 0 <= pair < pairs(done):
+                    turned.append(turn_xw(done, pair))
             for grouped, codes, scales in turned:
                 quantise(grouped, codes, scales)
             for k, g, w_codes, w_scales in quantised.get(rnd - LAG, []):
@@ -267,16 +293,17 @@ def tile_infonceloss_pa_k_kernel(tc, embeddings, contexts, W, out):
             for done in sorted(closed_in):
                 if rnd == closed_in[done]:
                     round_xw(done)
-                since_turned = rnd - closed_in[done] - (TIMES - done)
+                since_turned = rnd - closed_in[done] - pairs(done)
                 if since_turned == 1:
                     score(done)
                 if since_turned == 2:
                     exponentials(done)
                 if since_turned == 3:
                     logarithm(done)
+                    diagonal(done)
                 if since_turned == 4:
-                    spread_loss(done)
+                    place_loss(done)
                 if since_turned == 5:
-                    flatten(done)
+                    gather(done)
                 if since_turned == 6:
                     store(done)

from contextlib import ExitStack

import concourse.mybir as mybir
from concourse.masks import make_identity

F32 = mybir.dt.float32
BF16 = mybir.dt.bfloat16
U32 = mybir.dt.uint32
U8 = mybir.dt.uint8
FP8X4 = mybir.dt.float8_e4m3fn_x4
ACT = mybir.ActivationFunctionType
ALU = mybir.AluOpType
AXIS = mybir.AxisListType

P = 128
DX = 8192
DY = 512
STEPS = 3
TIMES = 4
PACK = 4
K_PASS = P * PACK
PASSES = DX // K_PASS
BLOCKS = 4
ROWS = BLOCKS * P
LOAD_PASSES = 2
LOAD_D = LOAD_PASSES * K_PASS
PASS_WORDS = K_PASS // 2
LAG = 2
GATHER = 8

FLOPS = 2 * (4 + 3 + 2) * P * DY * DX + 2 * (4 + 3 + 2) * P * P * DY
BYTES = 2 * (P * TIMES * DX + P * TIMES * DY + STEPS * DY * DX) + 4 * (4 + 3 + 2) * P


def tile_infonceloss_pa_k_kernel(tc, embeddings, contexts, W, out):
    nc = tc.nc
    with ExitStack() as ctx:
        consts = ctx.enter_context(tc.tile_pool(name="consts", bufs=1))
        keep = ctx.enter_context(tc.tile_pool(name="keep", bufs=1))
        x_loads = ctx.enter_context(tc.tile_pool(name="x_loads", bufs=3))
        w_loads = ctx.enter_context(tc.tile_pool(name="w_loads", bufs=8))
        stage = ctx.enter_context(tc.tile_pool(name="stage", bufs=4))
        w_mx = ctx.enter_context(tc.tile_pool(name="w_mx", bufs=2 * (LAG + 2)))
        second = ctx.enter_context(tc.tile_pool(name="second", bufs=2))
        xw_rows = ctx.enter_context(tc.tile_pool(name="xw_rows", bufs=TIMES))
        e_stage = ctx.enter_context(tc.tile_pool(name="e_stage", bufs=2))
        sums_psum = ctx.enter_context(tc.psum_pool(name="sums_psum", bufs=1))
        work_psum = ctx.enter_context(tc.psum_pool(name="work_psum", bufs=4))
        ctx.enter_context(tc.manual_schedule())

        ident_f32 = consts.tile([P, P], F32)
        make_identity(nc, ident_f32[:])
        ident_bf16 = consts.tile([P, P], BF16)
        make_identity(nc, ident_bf16[:])
        group = consts.tile([P, P], F32)
        nc.vector.memset(group[:], 0.0)
        nc.vector.tensor_reduce(
            out=group[:, 0 : P // GATHER],
            in_=ident_f32[:].rearrange("p (h l) -> p h l", l=GATHER),
            axis=AXIS.X,
            op=ALU.add,
        )
        place = consts.tile([P, GATHER], F32)
        nc.vector.tensor_reduce(
            out=place[:], in_=ident_f32[:].rearrange("p (h l) -> p l h", l=GATHER), axis=AXIS.X, op=ALU.add
        )
        warm = consts.tile([P, 1], F32)
        nc.scalar.activation(out=warm[:], in_=place[:, 0:1], func=ACT.Exp)

        def load_rows(pool, rows_view, load):
            raw = pool.tile([P, BLOCKS * LOAD_D], BF16, tag="raw")
            nc.sync.dma_start(
                out=raw[:].rearrange("p (r d) -> p r d", r=BLOCKS),
                in_=rows_view[:, :, load * LOAD_D : (load + 1) * LOAD_D],
            )
            return raw

        def turn_pass(raw, g, vector_copies_last):
            words = raw[:].bitcast(F32)
            grouped = stage.tile([P, ROWS * PACK], BF16, tag="grouped", align_bytes=64)
            grouped_words = grouped[:].bitcast(F32).rearrange("p (c u) -> p c u", u=2)
            for half in range(2):
                bank = work_psum.tile([P, 2, 2 * P], F32, tag="work")
                for blk in range(2):
                    for u in range(2):
                        first = ((2 * half + blk) * LOAD_PASSES + g % LOAD_PASSES) * PASS_WORDS + u * P
                        nc.tensor.transpose(
                            bank[:, u, blk * P : (blk + 1) * P], words[:, first : first + P], ident_f32[:]
                        )
                side_by_side = grouped_words[:, half * 2 * P : (half + 1) * 2 * P, :]
                if half == 1 and vector_copies_last:
                    nc.vector.tensor_copy(out=side_by_side, in_=bank[:].rearrange("p u c -> p c u"))
                else:
                    nc.scalar.copy(out=side_by_side, in_=bank[:].rearrange("p u c -> p c u"))
            return grouped

        def quantise(grouped, codes, scales):
            nc.vector.quantize_mx(out=codes.bitcast(FP8X4), scales=scales, in_=grouped[:])

        def turn_rows(rows_list, bank, on_scalar):
            n = len(rows_list)
            turned = sums_psum.tile([P, n, PACK, P], BF16, tag=bank)
            for i in range(n):
                for t in range(PACK):
                    nc.tensor.transpose(turned[:, i, t, :], rows_list[i][:, t * P : (t + 1) * P], ident_bf16[:])
            grouped = e_stage.tile([P, n * P * PACK], BF16, tag="grouped_e", align_bytes=64)
            side_by_side = grouped[:].rearrange("p (i r t) -> p i r t", i=n, t=PACK)
            if on_scalar:
                nc.scalar.copy(out=side_by_side, in_=turned[:].rearrange("p i t r -> p i r t"))
            else:
                nc.vector.tensor_copy(out=side_by_side, in_=turned[:].rearrange("p i t r -> p i r t"))
            return grouped

        def own_bank(k):
            return "sums%d" % (TIMES - 1 - k)

        def pairs(k):
            return (TIMES - k + 1) // 2

        xw = {}
        xw_codes = {}
        xw_scales = {}
        scores = {}
        top = {}
        minus_top = {}
        top_less_positive = {}
        exp_sums = {}
        log_mean = {}
        placed = {}
        gathered = {}

        def round_xw(k):
            xw_codes[k] = second.tile([P, TIMES * P], U32, tag="xw_codes", align_bytes=64, name="xw_codes_%d" % k)
            xw_scales[k] = second.tile([P, TIMES * P], U8, tag="xw_scales", align_bytes=64, name="xw_scales_%d" % k)
            for s in range(TIMES - k):
                xw[(k, s)] = xw_rows.tile([P, DY], BF16, tag="xw", name="xw_%d_%d" % (k, s))
                if s % 2 == 0:
                    nc.scalar.copy(out=xw[(k, s)][:], in_=sums[(k, s)][:])
                else:
                    nc.vector.tensor_copy(out=xw[(k, s)][:], in_=sums[(k, s)][:])

        def turn_xw(k, pair):
            times = range(2 * pair, min(2 * pair + 2, TIMES - k))
            cols = slice(times[0] * P, (times[-1] + 1) * P)
            grouped = turn_rows([xw[(k, s)] for s in times], own_bank(k), pair % 2 == 1)
            return (grouped, xw_codes[k][:, cols], xw_scales[k][:, cols])

        def score(k):
            n_s = TIMES - k
            scores[k] = sums_psum.tile([P, n_s, P], F32, tag=own_bank(k), name="scores_%d" % k)
            for s in range(n_s):
                cols = slice(s * P, (s + 1) * P)
                nc.tensor.matmul_mx(
                    out=scores[k][:, s, :],
                    lhsT=xw_codes[k][:, cols].bitcast(FP8X4),
                    lhsT_scale=xw_scales[k][:, cols],
                    rhs=c_codes[:, cols].bitcast(FP8X4),
                    rhs_scale=c_scales[:, cols],
                    start=True,
                    stop=True,
                )
            top[k] = second.tile([P, n_s], F32, tag="top", name="top_%d" % k)
            nc.vector.tensor_reduce(out=top[k][:], in_=scores[k][:], axis=AXIS.X, op=ALU.max)
            minus_top[k] = second.tile([P, n_s], F32, tag="minus_top", name="minus_top_%d" % k)
            nc.vector.tensor_scalar_mul(out=minus_top[k][:], in0=top[k][:], scalar1=-1.0)

        def diagonal(k):
            n_s = TIMES - k
            on_diagonal = second.tile([P, n_s, P], F32, tag="on_diagonal")
            nc.vector.tensor_tensor(
                out=on_diagonal[:],
                in0=scores[k][:],
                in1=ident_f32[:].unsqueeze(1).to_broadcast([P, n_s, P]),
                op=ALU.mult,
            )
            positive = second.tile([P, n_s], F32, tag="positive")
            nc.vector.tensor_reduce(out=positive[:], in_=on_diagonal[:], axis=AXIS.X, op=ALU.add)
            top_less_positive[k] = second.tile([P, n_s], F32, tag="top_less_positive", name="tlp_%d" % k)
            nc.vector.tensor_sub(out=top_less_positive[k][:], in0=top[k][:], in1=positive[:])

        def exponentials(k):
            n_s = TIMES - k
            exps = second.tile([P, n_s, P], F32, tag="exps")
            exp_sums[k] = second.tile([P, n_s], F32, tag="exp_sums", name="exp_sums_%d" % k)
            for s in range(n_s):
                nc.scalar.activation(
                    out=exps[:, s, :],
                    in_=scores[k][:, s, :],
                    func=ACT.Exp,
                    bias=minus_top[k][:, s : s + 1],
                    scale=1.0,
                    accum_out=exp_sums[k][:, s : s + 1],
                )

        def logarithm(k):
            n_s = TIMES - k
            log_mean[k] = second.tile([P, n_s], F32, tag="log_mean", name="log_mean_%d" % k)
            nc.scalar.activation(out=log_mean[k][:], in_=exp_sums[k][:], func=ACT.Ln, scale=1.0 / (P * n_s))

        def place_loss(k):
            n_s = TIMES - k
            loss = second.tile([P, n_s], F32, tag="loss")
            nc.vector.tensor_add(out=loss[:], in0=log_mean[k][:], in1=top_less_positive[k][:])
            placed[k] = second.tile([P, GATHER, n_s], F32, tag="placed", name="placed_%d" % k)
            nc.vector.tensor_tensor(
                out=placed[k][:],
                in0=place[:].unsqueeze(2).to_broadcast([P, GATHER, n_s]),
                in1=loss[:].unsqueeze(1).to_broadcast([P, GATHER, n_s]),
                op=ALU.mult,
            )

        def gather(k):
            gathered[k] = sums_psum.tile([P, GATHER * (TIMES - k)], F32, tag=own_bank(k), name="gathered_%d" % k)
            nc.tensor.matmul(
                out=gathered[k][:], lhsT=group[:], rhs=placed[k][:].rearrange("p l s -> p (l s)"), start=True, stop=True
            )

        def store(k):
            groups = P // GATHER
            n = GATHER * (TIMES - k)
            runs = second.tile([groups, n], F32, tag="runs")
            nc.scalar.copy(out=runs[:], in_=gathered[k][0:groups, :])
            first = sum(P * (TIMES - j) for j in range(k))
            nc.scalar.dma_start(out=out[first : first + groups * n].rearrange("(h n) -> h n", h=groups), in_=runs[:])

        c_raw = keep.tile([P, TIMES * DY], BF16)
        nc.sync.dma_start(out=c_raw[:].rearrange("p (t e) -> p t e", t=TIMES), in_=contexts[:, 0:TIMES, :])
        c_codes = keep.tile([P, TIMES * P], U32, align_bytes=64)
        c_scales = keep.tile([P, TIMES * P], U8, align_bytes=64)
        c_rows = [c_raw[:, s * DY : (s + 1) * DY] for s in range(TIMES)]
        c_turned = [turn_rows(c_rows[2 * pair : 2 * pair + 2], "sums%d" % pair, pair % 2 == 1) for pair in range(2)]
        for pair in range(2):
            cols = slice(2 * pair * P, 2 * (pair + 1) * P)
            quantise(c_turned[pair], c_codes[:, cols], c_scales[:, cols])

        x_view = embeddings[:, 1 : 1 + TIMES, :]
        x_codes = keep.tile([P, PASSES * ROWS], U32, align_bytes=64)
        x_scales = keep.tile([P, PASSES * ROWS], U8, align_bytes=64)
        sums = {}

        def multiply(k, g, w_codes, w_scales):
            for s in range(TIMES - k):
                if g == 0:
                    sums[(k, s)] = sums_psum.tile([P, DY], F32, tag="sums%d" % s, name="sums_%d_%d" % (k, s))
                cols = slice(g * ROWS + (k + s) * P, g * ROWS + (k + s + 1) * P)
                nc.tensor.matmul_mx(
                    out=sums[(k, s)][:],
                    lhsT=x_codes[:, cols].bitcast(FP8X4),
                    lhsT_scale=x_scales[:, cols],
                    rhs=w_codes[:].bitcast(FP8X4),
                    rhs_scale=w_scales[:],
                    start=(g == 0),
                    stop=(g == PASSES - 1),
                )

        plan = []
        for k in range(STEPS):
            w_passes = 1 if k == 0 else 2
            for first in range(0, PASSES, w_passes):
                plan.append((k, range(first, first + w_passes)))

        quantised = {}
        closed_in = {}
        for rnd in range(len(plan) + LAG + TIMES + 7):
            turned = []
            quantised[rnd] = []
            if rnd < len(plan):
                k, w_passes = plan[rnd]
                if k == 0:
                    g = rnd
                    if g % LOAD_PASSES == 0:
                        x_raw = load_rows(x_loads, x_view, g // LOAD_PASSES)
                    cols = slice(g * ROWS, (g + 1) * ROWS)
                    turned.append((turn_pass(x_raw, g, False), x_codes[:, cols], x_scales[:, cols]))
                for g in w_passes:
                    if g % LOAD_PASSES == 0:
                        w_view = W[k].rearrange("(r p) d -> p r d", p=P)
                        w_raw = load_rows(w_loads, w_view, g // LOAD_PASSES)
                    w_codes = w_mx.tile([P, ROWS], U32, tag="w_codes", align_bytes=64)
                    w_scales = w_mx.tile([P, ROWS], U8, tag="w_scales", align_bytes=64)
                    turned.append((turn_pass(w_raw, g, len(turned) == 1), w_codes[:], w_scales[:]))
                    quantised[rnd].append((k, g, w_codes, w_scales))
            for done in sorted(closed_in):
                pair = rnd - closed_in[done] - 1
                if 0 <= pair < pairs(done):
                    turned.append(turn_xw(done, pair))
            for grouped, codes, scales in turned:
                quantise(grouped, codes, scales)
            for k, g, w_codes, w_scales in quantised.get(rnd - LAG, []):
                multiply(k, g, w_codes, w_scales)
                if g == PASSES - 1:
                    closed_in[k] = rnd
            for done in sorted(closed_in):
                if rnd == closed_in[done]:
                    round_xw(done)
                since_turned = rnd - closed_in[done] - pairs(done)
                if since_turned == 1:
                    score(done)
                if since_turned == 2:
                    exponentials(done)
                if since_turned == 3:
                    logarithm(done)
                    diagonal(done)
                if since_turned == 4:
                    place_loss(done)
                if since_turned == 5:
                    gather(done)
                if since_turned == 6:
                    store(done)
